import numpy as np
import ml_dtypes

BF16 = ml_dtypes.bfloat16


def bf(x):
    return np.asarray(x, np.float32).astype(BF16)


def f32(x):
    return np.asarray(x, np.float32)


def f64(x):
    return np.asarray(x).astype(np.float64)


def striped(idx):
    return np.tile(idx.reshape(-1, 16).T, (8, 1))


C, S, N, GATES = 512, 1024, 256, 3


def sigmoid(v):
    return 1.0 / (1.0 + np.exp(-v))


def setup_inputs():
    return {"base": f32(np.random.standard_normal((C, S))), "x": bf(np.random.standard_normal((C, N))), "h": bf(np.random.standard_normal((C, N))), "w_ih": bf(np.random.standard_normal((C, GATES * C)) / np.sqrt(C)), "w_hh": bf(np.random.standard_normal((C, GATES * C)) / np.sqrt(C)), "b_ih": f32(0.2 * np.random.standard_normal((GATES * C, 1))), "b_hh": f32(0.2 * np.random.standard_normal((GATES * C, 1))), "offs": striped(np.random.permutation(S)[:N])}


def reference(base, x, h, w_ih, w_hh, b_ih, b_hh, offs):
    idx = offs[:16].T.reshape(-1)
    i_r, i_z, i_n = (f64(w_ih).T @ f64(x) + f64(b_ih)).reshape(GATES, C, N)
    h_r, h_z, h_n = (f64(w_hh).T @ f64(h) + f64(b_hh)).reshape(GATES, C, N)
    r = sigmoid(i_r + h_r)
    z = sigmoid(i_z + h_z)
    cand = np.tanh(i_n + r * h_n)
    out = f64(base).copy()
    out[:, idx] = (1.0 - z) * cand + z * f64(h)
    return out

@@ -1,0 +1,115 @@
+import concourse.mybir as mybir
+from concourse.masks import make_identity
+
+F32 = mybir.dt.float32
+BF16 = mybir.dt.bfloat16
+U16 = mybir.dt.uint16
+ADD = mybir.AluOpType.add
+MULT = mybir.AluOpType.mult
+SIGMOID = mybir.ActivationFunctionType.Sigmoid
+TANH = mybir.ActivationFunctionType.Tanh
+
+P = 128
+C = 512
+S = 1024
+N = 256
+BLOCKS = C // P
+R = 0
+Z = 1
+CAND = 2
+GATES = 3
+
+FLOPS = 2 * 2 * C * GATES * C * N
+
+
+def tile_mem2seq_kernel(tc, base, x, h, w_ih, w_hh, b_ih, b_hh, offs, out):
+    nc = tc.nc
+    with (
+        tc.tile_pool(name="held", bufs=1) as held,
+        tc.tile_pool(name="work", bufs=2) as work,
+    ):
+        offsets = held.tile([P, N // 16], U16, name="offsets")
+        nc.sync.dma_start(offsets[:], offs)
+        x_sb = held.tile([P, BLOCKS, N], BF16, name="x_sb")
+        nc.sync.dma_start(x_sb[:], x.rearrange("(kb p) n -> p kb n", p=P))
+        h_sb = held.tile([P, BLOCKS, N], BF16, name="h_sb")
+        nc.sync.dma_start(h_sb[:], h.rearrange("(kb p) n -> p kb n", p=P))
+        w_ih_sb = []
+        w_hh_sb = []
+        for w_dram, w_list, label in ((w_ih, w_ih_sb, "w_ih"), (w_hh, w_hh_sb, "w_hh")):
+            for kb in range(BLOCKS):
+                w_rows = held.tile([P, GATES * C], BF16, name=f"{label}_{kb}")
+                nc.sync.dma_start(w_rows[:], w_dram[kb * P : (kb + 1) * P, :])
+                w_list.append(w_rows)
+        windows = []
+        for cb in range(BLOCKS):
+            window = held.tile([P, S], F32, name=f"window_{cb}")
+            nc.sync.dma_start(window[:], base[cb * P : (cb + 1) * P, :])
+            windows.append(window)
+
+        bias_rows = held.tile([P, P], F32, name="bias_rows")
+        nc.vector.memset(bias_rows[:], 0.0)
+        rows = GATES * BLOCKS
+        nc.scalar.dma_start(bias_rows[0:rows, :], b_ih.rearrange("(g p) o -> g (p o)", p=P))
+        nc.scalar.dma_start(bias_rows[rows : 2 * rows, :], b_hh.rearrange("(g p) o -> g (p o)", p=P))
+        identity = held.tile([P, P], F32, name="identity")
+        make_identity(nc, identity[:])
+        bias_cols = held.tile([P, 2 * rows], F32, name="bias_cols")
+        with tc.psum_pool(name="setup_psum", bufs=1) as setup_psum:
+            bias_ps = setup_psum.tile([P, P], F32, name="bias_ps")
+            nc.tensor.transpose(bias_ps[:], bias_rows[:], identity[:])
+            nc.vector.tensor_copy(bias_cols[:], bias_ps[:, 0 : 2 * rows])
+        b_rz = held.tile([P, 2 * BLOCKS], F32, name="b_rz")
+        nc.vector.tensor_tensor(b_rz[:], bias_cols[:, 0 : 2 * BLOCKS], bias_cols[:, rows : rows + 2 * BLOCKS], ADD)
+        neg_b_z = held.tile([P, BLOCKS], F32, name="neg_b_z")
+        nc.vector.tensor_scalar_mul(neg_b_z[:], b_rz[:, BLOCKS : 2 * BLOCKS], -1.0)
+
+        with tc.psum_pool(name="psum", bufs=2) as psum:
+            for cb in range(BLOCKS):
+
+                def columns(gate):
+                    return slice(gate * C + cb * P, gate * C + (cb + 1) * P)
+
+                ps_r = psum.tile([P, N], F32, name="ps_r")
+                ps_z = psum.tile([P, N], F32, name="ps_z")
+                for acc, gate in ((ps_r, R), (ps_z, Z)):
+                    for kb in range(BLOCKS):
+                        nc.tensor.matmul(acc[:], w_ih_sb[kb][:, columns(gate)], x_sb[:, kb, :], start=(kb == 0), stop=False)
+                    for kb in range(BLOCKS):
+                        nc.tensor.matmul(
+                            acc[:], w_hh_sb[kb][:, columns(gate)], h_sb[:, kb, :], start=False, stop=(kb == BLOCKS - 1)
+                        )
+                ps_hn = psum.tile([P, N], F32, name="ps_hn")
+                for kb in range(BLOCKS):
+                    nc.tensor.matmul(
+                        ps_hn[:], w_hh_sb[kb][:, columns(CAND)], h_sb[:, kb, :], start=(kb == 0), stop=(kb == BLOCKS - 1)
+                    )
+                ps_in = psum.tile([P, N], F32, name="ps_in")
+                for kb in range(BLOCKS):
+                    nc.tensor.matmul(
+                        ps_in[:], w_ih_sb[kb][:, columns(CAND)], x_sb[:, kb, :], start=(kb == 0), stop=(kb == BLOCKS - 1)
+                    )
+
+                b_r = b_rz[:, cb : cb + 1]
+                b_z = b_rz[:, BLOCKS + cb : BLOCKS + cb + 1]
+                b_in = bias_cols[:, CAND * BLOCKS + cb : CAND * BLOCKS + cb + 1]
+                b_hn = bias_cols[:, rows + CAND * BLOCKS + cb : rows + CAND * BLOCKS + cb + 1]
+                r = work.tile([P, N], F32, name="r")
+                nc.scalar.activation(r[:], ps_r[:], SIGMOID, bias=b_r)
+                z = work.tile([P, N], F32, name="z")
+                nc.scalar.activation(z[:], ps_z[:], SIGMOID, bias=b_z)
+                one_minus_z = work.tile([P, N], F32, name="one_minus_z")
+                nc.scalar.activation(one_minus_z[:], ps_z[:], SIGMOID, bias=neg_b_z[:, cb : cb + 1], scale=-1.0)
+                r_hn = work.tile([P, N], F32, name="r_hn")
+                nc.vector.scalar_tensor_tensor(r_hn[:], ps_hn[:], b_hn, r[:], op0=ADD, op1=MULT)
+                pre_cand = work.tile([P, N], F32, name="pre_cand")
+                nc.vector.tensor_tensor(pre_cand[:], r_hn[:], ps_in[:], ADD)
+                cand = work.tile([P, N], F32, name="cand")
+                nc.scalar.activation(cand[:], pre_cand[:], TANH, bias=b_in)
+
+                kept = work.tile([P, N], F32, name="kept")
+                nc.vector.tensor_tensor(kept[:], z[:], h_sb[:, cb, :], MULT)
+                fresh = work.tile([P, N], F32, name="fresh")
+                nc.vector.tensor_tensor(fresh[:], one_minus_z[:], cand[:], MULT)
+                nc.vector.tensor_tensor(windows[cb][:].indirect(offsets[:]), fresh[:], kept[:], ADD)
+                nc.sync.dma_start(out[cb * P : (cb + 1) * P, :], windows[cb][:])

@@ -28,88 +28,101 @@ def tile_mem2seq_kernel(tc, base, x, h, w_ih, w_hh, b_ih, b_hh, offs, out):
         tc.tile_pool(name="held", bufs=1) as held,
         tc.tile_pool(name="work", bufs=2) as work,
     ):
+        moving_dram = {"ih": x, "hh": h}
+        w_dram = {"ih": w_ih, "hh": w_hh}
+        moving = {}
+        weights = {}
         offsets = held.tile([P, N // 16], U16, name="offsets")
-        nc.sync.dma_start(offsets[:], offs)
-        x_sb = held.tile([P, BLOCKS, N], BF16, name="x_sb")
-        nc.sync.dma_start(x_sb[:], x.rearrange("(kb p) n -> p kb n", p=P))
-        h_sb = held.tile([P, BLOCKS, N], BF16, name="h_sb")
-        nc.sync.dma_start(h_sb[:], h.rearrange("(kb p) n -> p kb n", p=P))
-        w_ih_sb = []
-        w_hh_sb = []
-        for w_dram, w_list, label in ((w_ih, w_ih_sb, "w_ih"), (w_hh, w_hh_sb, "w_hh")):
-            for kb in range(BLOCKS):
-                w_rows = held.tile([P, GATES * C], BF16, name=f"{label}_{kb}")
-                nc.sync.dma_start(w_rows[:], w_dram[kb * P : (kb + 1) * P, :])
-                w_list.append(w_rows)
-        windows = []
-        for cb in range(BLOCKS):
-            window = held.tile([P, S], F32, name=f"window_{cb}")
-            nc.sync.dma_start(window[:], base[cb * P : (cb + 1) * P, :])
-            windows.append(window)
-
-        bias_rows = held.tile([P, P], F32, name="bias_rows")
-        nc.vector.memset(bias_rows[:], 0.0)
         rows = GATES * BLOCKS
-        nc.scalar.dma_start(bias_rows[0:rows, :], b_ih.rearrange("(g p) o -> g (p o)", p=P))
-        nc.scalar.dma_start(bias_rows[rows : 2 * rows, :], b_hh.rearrange("(g p) o -> g (p o)", p=P))
-        identity = held.tile([P, P], F32, name="identity")
-        make_identity(nc, identity[:])
-        bias_cols = held.tile([P, 2 * rows], F32, name="bias_cols")
-        with tc.psum_pool(name="setup_psum", bufs=1) as setup_psum:
-            bias_ps = setup_psum.tile([P, P], F32, name="bias_ps")
-            nc.tensor.transpose(bias_ps[:], bias_rows[:], identity[:])
-            nc.vector.tensor_copy(bias_cols[:], bias_ps[:, 0 : 2 * rows])
-        b_rz = held.tile([P, 2 * BLOCKS], F32, name="b_rz")
-        nc.vector.tensor_tensor(b_rz[:], bias_cols[:, 0 : 2 * BLOCKS], bias_cols[:, rows : rows + 2 * BLOCKS], ADD)
-        neg_b_z = held.tile([P, BLOCKS], F32, name="neg_b_z")
-        nc.vector.tensor_scalar_mul(neg_b_z[:], b_rz[:, BLOCKS : 2 * BLOCKS], -1.0)
+        bias_rows = held.tile([2 * rows, P], F32, name="bias_rows")
+        windows = [held.tile([P, S], F32, name=f"window_{cb}") for cb in range(BLOCKS)]
+        for pair in range(BLOCKS // 2):
+            for name, gate in (("ih", R), ("hh", R), ("hh", CAND), ("ih", Z), ("hh", Z), ("ih", CAND)):
+                if name not in moving:
+                    moving[name] = held.tile([P, BLOCKS, N], BF16, name=f"moving_{name}")
+                    nc.sync.dma_start(moving[name][:], moving_dram[name].rearrange("(kb p) n -> p kb n", p=P))
+                w_slice = held.tile([P, BLOCKS, 2 * P], BF16, name=f"w_{name}_{gate}_{pair}")
+                first = gate * C + pair * 2 * P
+                nc.sync.dma_start(
+                    w_slice[:], w_dram[name][:, first : first + 2 * P].rearrange("(kb p) m -> p kb m", p=P)
+                )
+                weights[name, gate, pair] = w_slice
+                if (pair, name, gate) == (0, "ih", R):
+                    for b_dram, at in ((b_ih, 0), (b_hh, rows)):
+                        b_rows = b_dram.rearrange("(g p) o -> g (p o)", p=P)
+                        nc.sync.dma_start(bias_rows[at : at + 8, :], b_rows[0:8, :])
+                        nc.sync.dma_start(bias_rows[at + 8 : at + rows, :], b_rows[8:rows, :])
+            if pair == 0:
+                nc.sync.dma_start(offsets[:], offs)
+            for cb in (2 * pair, 2 * pair + 1):
+                nc.sync.dma_start(windows[cb][:], base[cb * P : (cb + 1) * P, :])
 
-        with tc.psum_pool(name="psum", bufs=2) as psum:
-            for cb in range(BLOCKS):
+        with tc.psum_pool(name="psum", bufs=1) as psum:
+            identity = held.tile([2 * rows, 2 * rows], F32, name="identity")
+            make_identity(nc, identity[:])
+            bias_ps = psum.tile([P, 2 * rows], F32, name="bias_ps")
+            nc.tensor.matmul(bias_ps[:], bias_rows[:], identity[:], start=True, stop=True)
+            bias_cols = held.tile([P, 2 * rows], F32, name="bias_cols")
+            nc.vector.tensor_copy(bias_cols[:], bias_ps[:])
+            b_rz = held.tile([P, 2 * BLOCKS], F32, name="b_rz")
+            nc.vector.tensor_tensor(b_rz[:], bias_cols[:, 0 : 2 * BLOCKS], bias_cols[:, rows : rows + 2 * BLOCKS], ADD)
+            neg_b_z = held.tile([P, BLOCKS], F32, name="neg_b_z")
+            nc.vector.tensor_scalar_mul(neg_b_z[:], b_rz[:, BLOCKS : 2 * BLOCKS], -1.0)
 
-                def columns(gate):
-                    return slice(gate * C + cb * P, gate * C + (cb + 1) * P)
-
+            def new_accumulators():
                 ps_r = psum.tile([P, N], F32, name="ps_r")
                 ps_z = psum.tile([P, N], F32, name="ps_z")
-                for acc, gate in ((ps_r, R), (ps_z, Z)):
-                    for kb in range(BLOCKS):
-                        nc.tensor.matmul(acc[:], w_ih_sb[kb][:, columns(gate)], x_sb[:, kb, :], start=(kb == 0), stop=False)
-                    for kb in range(BLOCKS):
-                        nc.tensor.matmul(
-                            acc[:], w_hh_sb[kb][:, columns(gate)], h_sb[:, kb, :], start=False, stop=(kb == BLOCKS - 1)
-                        )
-                ps_hn = psum.tile([P, N], F32, name="ps_hn")
-                for kb in range(BLOCKS):
-                    nc.tensor.matmul(
-                        ps_hn[:], w_hh_sb[kb][:, columns(CAND)], h_sb[:, kb, :], start=(kb == 0), stop=(kb == BLOCKS - 1)
-                    )
                 ps_in = psum.tile([P, N], F32, name="ps_in")
-                for kb in range(BLOCKS):
-                    nc.tensor.matmul(
-                        ps_in[:], w_ih_sb[kb][:, columns(CAND)], x_sb[:, kb, :], start=(kb == 0), stop=(kb == BLOCKS - 1)
-                    )
+                ps_hn = psum.tile([P, N], F32, name="ps_hn")
+                return {"r": ps_r, "z": ps_z, "in": ps_in, "hn": ps_hn}
 
+            def multiply(acc, name, gate, cb, kb, start, stop):
+                half = cb % 2
+                nc.tensor.matmul(
+                    acc[:],
+                    weights[name, gate, cb // 2][:, kb, half * P : (half + 1) * P],
+                    moving[name][:, kb, :],
+                    start=start,
+                    stop=stop,
+                )
+
+            def finish_block(cb, acc):
                 b_r = b_rz[:, cb : cb + 1]
                 b_z = b_rz[:, BLOCKS + cb : BLOCKS + cb + 1]
                 b_in = bias_cols[:, CAND * BLOCKS + cb : CAND * BLOCKS + cb + 1]
                 b_hn = bias_cols[:, rows + CAND * BLOCKS + cb : rows + CAND * BLOCKS + cb + 1]
                 r = work.tile([P, N], F32, name="r")
-                nc.scalar.activation(r[:], ps_r[:], SIGMOID, bias=b_r)
+                nc.scalar.activation(r[:], acc["r"][:], SIGMOID, bias=b_r)
                 z = work.tile([P, N], F32, name="z")
-                nc.scalar.activation(z[:], ps_z[:], SIGMOID, bias=b_z)
+                nc.scalar.activation(z[:], acc["z"][:], SIGMOID, bias=b_z)
                 one_minus_z = work.tile([P, N], F32, name="one_minus_z")
-                nc.scalar.activation(one_minus_z[:], ps_z[:], SIGMOID, bias=neg_b_z[:, cb : cb + 1], scale=-1.0)
+                nc.scalar.activation(one_minus_z[:], acc["z"][:], SIGMOID, bias=neg_b_z[:, cb : cb + 1], scale=-1.0)
                 r_hn = work.tile([P, N], F32, name="r_hn")
-                nc.vector.scalar_tensor_tensor(r_hn[:], ps_hn[:], b_hn, r[:], op0=ADD, op1=MULT)
+                nc.vector.scalar_tensor_tensor(r_hn[:], acc["hn"][:], b_hn, r[:], op0=ADD, op1=MULT)
                 pre_cand = work.tile([P, N], F32, name="pre_cand")
-                nc.vector.tensor_tensor(pre_cand[:], r_hn[:], ps_in[:], ADD)
+                nc.vector.tensor_tensor(pre_cand[:], r_hn[:], acc["in"][:], ADD)
                 cand = work.tile([P, N], F32, name="cand")
                 nc.scalar.activation(cand[:], pre_cand[:], TANH, bias=b_in)
-
                 kept = work.tile([P, N], F32, name="kept")
-                nc.vector.tensor_tensor(kept[:], z[:], h_sb[:, cb, :], MULT)
+                nc.vector.tensor_tensor(kept[:], z[:], moving["hh"][:, cb, :], MULT)
                 fresh = work.tile([P, N], F32, name="fresh")
                 nc.vector.tensor_tensor(fresh[:], one_minus_z[:], cand[:], MULT)
                 nc.vector.tensor_tensor(windows[cb][:].indirect(offsets[:]), fresh[:], kept[:], ADD)
                 nc.sync.dma_start(out[cb * P : (cb + 1) * P, :], windows[cb][:])
+
+            last = BLOCKS - 1
+            for cb in range(BLOCKS):
+                acc = new_accumulators()
+                for kb in range(BLOCKS):
+                    multiply(acc["r"], "ih", R, cb, kb, start=(kb == 0), stop=False)
+                for kb in range(BLOCKS):
+                    multiply(acc["r"], "hh", R, cb, kb, start=False, stop=(kb == last))
+                for kb in range(BLOCKS):
+                    multiply(acc["hn"], "hh", CAND, cb, kb, start=(kb == 0), stop=(kb == last))
+                for kb in range(BLOCKS):
+                    multiply(acc["z"], "ih", Z, cb, kb, start=(kb == 0), stop=False)
+                for kb in range(BLOCKS):
+                    multiply(acc["z"], "hh", Z, cb, kb, start=False, stop=(kb == last))
+                for kb in range(BLOCKS):
+                    multiply(acc["in"], "ih", CAND, cb, kb, start=(kb == 0), stop=(kb == last))
+                finish_block(cb, acc)

@@ -18,6 +18,7 @@ R = 0
 Z = 1
 CAND = 2
 GATES = 3
+WARM_UP_MATMULS = 5
 
 FLOPS = 2 * 2 * C * GATES * C * N
 
@@ -58,6 +59,12 @@ def tile_mem2seq_kernel(tc, base, x, h, w_ih, w_hh, b_ih, b_hh, offs, out):
                 nc.sync.dma_start(windows[cb][:], base[cb * P : (cb + 1) * P, :])
 
         with tc.psum_pool(name="psum", bufs=1) as psum:
+            zeros = held.tile([P, 2 * N], BF16, name="zeros")
+            nc.vector.memset(zeros[:], 0.0)
+            warm_ps = psum.tile([P, 2 * N], F32, name="warm_ps")
+            for step in range(WARM_UP_MATMULS):
+                nc.tensor.matmul(warm_ps[:], zeros[:, 0:P], zeros[:], start=True, stop=True)
+
             identity = held.tile([2 * rows, 2 * rows], F32, name="identity")
             make_identity(nc, identity[:])
             bias_ps = psum.tile([P, 2 * rows], F32, name="bias_ps")
@@ -92,21 +99,24 @@ def tile_mem2seq_kernel(tc, base, x, h, w_ih, w_hh, b_ih, b_hh, offs, out):
                 b_in = bias_cols[:, CAND * BLOCKS + cb : CAND * BLOCKS + cb + 1]
                 b_hn = bias_cols[:, rows + CAND * BLOCKS + cb : rows + CAND * BLOCKS + cb + 1]
                 r = work.tile([P, N], F32, name="r")
-                nc.scalar.activation(r[:], acc["r"][:], SIGMOID, bias=b_r)
                 z = work.tile([P, N], F32, name="z")
-                nc.scalar.activation(z[:], acc["z"][:], SIGMOID, bias=b_z)
                 one_minus_z = work.tile([P, N], F32, name="one_minus_z")
-                nc.scalar.activation(one_minus_z[:], acc["z"][:], SIGMOID, bias=neg_b_z[:, cb : cb + 1], scale=-1.0)
                 r_hn = work.tile([P, N], F32, name="r_hn")
-                nc.vector.scalar_tensor_tensor(r_hn[:], acc["hn"][:], b_hn, r[:], op0=ADD, op1=MULT)
                 pre_cand = work.tile([P, N], F32, name="pre_cand")
-                nc.vector.tensor_tensor(pre_cand[:], r_hn[:], acc["in"][:], ADD)
                 cand = work.tile([P, N], F32, name="cand")
-                nc.scalar.activation(cand[:], pre_cand[:], TANH, bias=b_in)
                 kept = work.tile([P, N], F32, name="kept")
-                nc.vector.tensor_tensor(kept[:], z[:], moving["hh"][:, cb, :], MULT)
                 fresh = work.tile([P, N], F32, name="fresh")
-                nc.vector.tensor_tensor(fresh[:], one_minus_z[:], cand[:], MULT)
+                for cols in (slice(0, N // 2), slice(N // 2, N)):
+                    nc.scalar.activation(r[:, cols], acc["r"][:, cols], SIGMOID, bias=b_r)
+                    nc.vector.scalar_tensor_tensor(r_hn[:, cols], acc["hn"][:, cols], b_hn, r[:, cols], op0=ADD, op1=MULT)
+                    nc.scalar.activation(z[:, cols], acc["z"][:, cols], SIGMOID, bias=b_z)
+                    nc.scalar.activation(
+                        one_minus_z[:, cols], acc["z"][:, cols], SIGMOID, bias=neg_b_z[:, cb : cb + 1], scale=-1.0
+                    )
+                    nc.vector.tensor_tensor(kept[:, cols], z[:, cols], moving["hh"][:, cb, cols], MULT)
+                    nc.vector.tensor_tensor(pre_cand[:, cols], r_hn[:, cols], acc["in"][:, cols], ADD)
+                    nc.scalar.activation(cand[:, cols], pre_cand[:, cols], TANH, bias=b_in)
+                    nc.vector.tensor_tensor(fresh[:, cols], one_minus_z[:, cols], cand[:, cols], MULT)
                 nc.vector.tensor_tensor(windows[cb][:].indirect(offsets[:]), fresh[:], kept[:], ADD)
                 nc.sync.dma_start(out[cb * P : (cb + 1) * P, :], windows[cb][:])
 

@@ -18,7 +18,6 @@ R = 0
 Z = 1
 CAND = 2
 GATES = 3
-WARM_UP_MATMULS = 5
 
 FLOPS = 2 * 2 * C * GATES * C * N
 
@@ -31,6 +30,7 @@ def tile_mem2seq_kernel(tc, base, x, h, w_ih, w_hh, b_ih, b_hh, offs, out):
     ):
         moving_dram = {"ih": x, "hh": h}
         w_dram = {"ih": w_ih, "hh": w_hh}
+        queue = {"ih": nc.sync, "hh": nc.scalar}
         moving = {}
         weights = {}
         offsets = held.tile([P, N // 16], U16, name="offsets")
@@ -41,10 +41,10 @@ def tile_mem2seq_kernel(tc, base, x, h, w_ih, w_hh, b_ih, b_hh, offs, out):
             for name, gate in (("ih", R), ("hh", R), ("hh", CAND), ("ih", Z), ("hh", Z), ("ih", CAND)):
                 if name not in moving:
                     moving[name] = held.tile([P, BLOCKS, N], BF16, name=f"moving_{name}")
-                    nc.sync.dma_start(moving[name][:], moving_dram[name].rearrange("(kb p) n -> p kb n", p=P))
+                    queue[name].dma_start(moving[name][:], moving_dram[name].rearrange("(kb p) n -> p kb n", p=P))
                 w_slice = held.tile([P, BLOCKS, 2 * P], BF16, name=f"w_{name}_{gate}_{pair}")
                 first = gate * C + pair * 2 * P
-                nc.sync.dma_start(
+                queue[name].dma_start(
                     w_slice[:], w_dram[name][:, first : first + 2 * P].rearrange("(kb p) m -> p kb m", p=P)
                 )
                 weights[name, gate, pair] = w_slice
@@ -59,12 +59,6 @@ def tile_mem2seq_kernel(tc, base, x, h, w_ih, w_hh, b_ih, b_hh, offs, out):
                 nc.sync.dma_start(windows[cb][:], base[cb * P : (cb + 1) * P, :])
 
         with tc.psum_pool(name="psum", bufs=1) as psum:
-            zeros = held.tile([P, 2 * N], BF16, name="zeros")
-            nc.vector.memset(zeros[:], 0.0)
-            warm_ps = psum.tile([P, 2 * N], F32, name="warm_ps")
-            for step in range(WARM_UP_MATMULS):
-                nc.tensor.matmul(warm_ps[:], zeros[:, 0:P], zeros[:], start=True, stop=True)
-
             identity = held.tile([2 * rows, 2 * rows], F32, name="identity")
             make_identity(nc, identity[:])
             bias_ps = psum.tile([P, 2 * rows], F32, name="bias_ps")
@@ -99,24 +93,21 @@ def tile_mem2seq_kernel(tc, base, x, h, w_ih, w_hh, b_ih, b_hh, offs, out):
                 b_in = bias_cols[:, CAND * BLOCKS + cb : CAND * BLOCKS + cb + 1]
                 b_hn = bias_cols[:, rows + CAND * BLOCKS + cb : rows + CAND * BLOCKS + cb + 1]
                 r = work.tile([P, N], F32, name="r")
+                nc.scalar.activation(r[:], acc["r"][:], SIGMOID, bias=b_r)
                 z = work.tile([P, N], F32, name="z")
+                nc.scalar.activation(z[:], acc["z"][:], SIGMOID, bias=b_z)
                 one_minus_z = work.tile([P, N], F32, name="one_minus_z")
+                nc.scalar.activation(one_minus_z[:], acc["z"][:], SIGMOID, bias=neg_b_z[:, cb : cb + 1], scale=-1.0)
                 r_hn = work.tile([P, N], F32, name="r_hn")
+                nc.vector.scalar_tensor_tensor(r_hn[:], acc["hn"][:], b_hn, r[:], op0=ADD, op1=MULT)
                 pre_cand = work.tile([P, N], F32, name="pre_cand")
+                nc.vector.tensor_tensor(pre_cand[:], r_hn[:], acc["in"][:], ADD)
                 cand = work.tile([P, N], F32, name="cand")
+                nc.scalar.activation(cand[:], pre_cand[:], TANH, bias=b_in)
                 kept = work.tile([P, N], F32, name="kept")
+                nc.vector.tensor_tensor(kept[:], z[:], moving["hh"][:, cb, :], MULT)
                 fresh = work.tile([P, N], F32, name="fresh")
-                for cols in (slice(0, N // 2), slice(N // 2, N)):
-                    nc.scalar.activation(r[:, cols], acc["r"][:, cols], SIGMOID, bias=b_r)
-                    nc.vector.scalar_tensor_tensor(r_hn[:, cols], acc["hn"][:, cols], b_hn, r[:, cols], op0=ADD, op1=MULT)
-                    nc.scalar.activation(z[:, cols], acc["z"][:, cols], SIGMOID, bias=b_z)
-                    nc.scalar.activation(
-                        one_minus_z[:, cols], acc["z"][:, cols], SIGMOID, bias=neg_b_z[:, cb : cb + 1], scale=-1.0
-                    )
-                    nc.vector.tensor_tensor(kept[:, cols], z[:, cols], moving["hh"][:, cb, cols], MULT)
-                    nc.vector.tensor_tensor(pre_cand[:, cols], r_hn[:, cols], acc["in"][:, cols], ADD)
-                    nc.scalar.activation(cand[:, cols], pre_cand[:, cols], TANH, bias=b_in)
-                    nc.vector.tensor_tensor(fresh[:, cols], one_minus_z[:, cols], cand[:, cols], MULT)
+                nc.vector.tensor_tensor(fresh[:], one_minus_z[:], cand[:], MULT)
                 nc.vector.tensor_tensor(windows[cb][:].indirect(offsets[:]), fresh[:], kept[:], ADD)
                 nc.sync.dma_start(out[cb * P : (cb + 1) * P, :], windows[cb][:])
 

@@ -30,7 +30,6 @@ def tile_mem2seq_kernel(tc, base, x, h, w_ih, w_hh, b_ih, b_hh, offs, out):
     ):
         moving_dram = {"ih": x, "hh": h}
         w_dram = {"ih": w_ih, "hh": w_hh}
-        queue = {"ih": nc.sync, "hh": nc.scalar}
         moving = {}
         weights = {}
         offsets = held.tile([P, N // 16], U16, name="offsets")
@@ -41,10 +40,10 @@ def tile_mem2seq_kernel(tc, base, x, h, w_ih, w_hh, b_ih, b_hh, offs, out):
             for name, gate in (("ih", R), ("hh", R), ("hh", CAND), ("ih", Z), ("hh", Z), ("ih", CAND)):
                 if name not in moving:
                     moving[name] = held.tile([P, BLOCKS, N], BF16, name=f"moving_{name}")
-                    queue[name].dma_start(moving[name][:], moving_dram[name].rearrange("(kb p) n -> p kb n", p=P))
+                    nc.sync.dma_start(moving[name][:], moving_dram[name].rearrange("(kb p) n -> p kb n", p=P))
                 w_slice = held.tile([P, BLOCKS, 2 * P], BF16, name=f"w_{name}_{gate}_{pair}")
                 first = gate * C + pair * 2 * P
-                queue[name].dma_start(
+                nc.sync.dma_start(
                     w_slice[:], w_dram[name][:, first : first + 2 * P].rearrange("(kb p) m -> p kb m", p=P)
                 )
                 weights[name, gate, pair] = w_slice
@@ -93,21 +92,24 @@ def tile_mem2seq_kernel(tc, base, x, h, w_ih, w_hh, b_ih, b_hh, offs, out):
                 b_in = bias_cols[:, CAND * BLOCKS + cb : CAND * BLOCKS + cb + 1]
                 b_hn = bias_cols[:, rows + CAND * BLOCKS + cb : rows + CAND * BLOCKS + cb + 1]
                 r = work.tile([P, N], F32, name="r")
-                nc.scalar.activation(r[:], acc["r"][:], SIGMOID, bias=b_r)
                 z = work.tile([P, N], F32, name="z")
-                nc.scalar.activation(z[:], acc["z"][:], SIGMOID, bias=b_z)
                 one_minus_z = work.tile([P, N], F32, name="one_minus_z")
-                nc.scalar.activation(one_minus_z[:], acc["z"][:], SIGMOID, bias=neg_b_z[:, cb : cb + 1], scale=-1.0)
                 r_hn = work.tile([P, N], F32, name="r_hn")
-                nc.vector.scalar_tensor_tensor(r_hn[:], acc["hn"][:], b_hn, r[:], op0=ADD, op1=MULT)
                 pre_cand = work.tile([P, N], F32, name="pre_cand")
-                nc.vector.tensor_tensor(pre_cand[:], r_hn[:], acc["in"][:], ADD)
                 cand = work.tile([P, N], F32, name="cand")
-                nc.scalar.activation(cand[:], pre_cand[:], TANH, bias=b_in)
                 kept = work.tile([P, N], F32, name="kept")
-                nc.vector.tensor_tensor(kept[:], z[:], moving["hh"][:, cb, :], MULT)
                 fresh = work.tile([P, N], F32, name="fresh")
-                nc.vector.tensor_tensor(fresh[:], one_minus_z[:], cand[:], MULT)
+                for cols in (slice(0, N // 2), slice(N // 2, N)):
+                    nc.scalar.activation(r[:, cols], acc["r"][:, cols], SIGMOID, bias=b_r)
+                    nc.vector.scalar_tensor_tensor(r_hn[:, cols], acc["hn"][:, cols], b_hn, r[:, cols], op0=ADD, op1=MULT)
+                    nc.scalar.activation(z[:, cols], acc["z"][:, cols], SIGMOID, bias=b_z)
+                    nc.scalar.activation(
+                        one_minus_z[:, cols], acc["z"][:, cols], SIGMOID, bias=neg_b_z[:, cb : cb + 1], scale=-1.0
+                    )
+                    nc.vector.tensor_tensor(kept[:, cols], z[:, cols], moving["hh"][:, cb, cols], MULT)
+                    nc.vector.tensor_tensor(pre_cand[:, cols], r_hn[:, cols], acc["in"][:, cols], ADD)
+                    nc.scalar.activation(cand[:, cols], pre_cand[:, cols], TANH, bias=b_in)
+                    nc.vector.tensor_tensor(fresh[:, cols], one_minus_z[:, cols], cand[:, cols], MULT)
                 nc.vector.tensor_tensor(windows[cb][:].indirect(offsets[:]), fresh[:], kept[:], ADD)
                 nc.sync.dma_start(out[cb * P : (cb + 1) * P, :], windows[cb][:])
 

@@ -70,10 +70,10 @@ def tile_mem2seq_kernel(tc, base, x, h, w_ih, w_hh, b_ih, b_hh, offs, out):
             nc.vector.tensor_scalar_mul(neg_b_z[:], b_rz[:, BLOCKS : 2 * BLOCKS], -1.0)
 
             def new_accumulators():
-                ps_r = psum.tile([P, N], F32, name="ps_r")
-                ps_z = psum.tile([P, N], F32, name="ps_z")
+                ps_r = psum.tile([P, N], F32, name="ps_r", bufs=2)
+                ps_z = psum.tile([P, N], F32, name="ps_z", bufs=2)
                 ps_in = psum.tile([P, N], F32, name="ps_in")
-                ps_hn = psum.tile([P, N], F32, name="ps_hn")
+                ps_hn = psum.tile([P, N], F32, name="ps_hn", bufs=2)
                 return {"r": ps_r, "z": ps_z, "in": ps_in, "hn": ps_hn}
 
             def multiply(acc, name, gate, cb, kb, start, stop):

@@ -57,10 +57,10 @@ def tile_mem2seq_kernel(tc, base, x, h, w_ih, w_hh, b_ih, b_hh, offs, out):
             for cb in (2 * pair, 2 * pair + 1):
                 nc.sync.dma_start(windows[cb][:], base[cb * P : (cb + 1) * P, :])
 
-        with tc.psum_pool(name="psum", bufs=1) as psum:
+        with tc.psum_pool(name="psum", bufs=2) as psum:
             identity = held.tile([2 * rows, 2 * rows], F32, name="identity")
             make_identity(nc, identity[:])
-            bias_ps = psum.tile([P, 2 * rows], F32, name="bias_ps")
+            bias_ps = psum.tile([P, 2 * rows], F32, name="bias_ps", tag="ps_in")
             nc.tensor.matmul(bias_ps[:], bias_rows[:], identity[:], start=True, stop=True)
             bias_cols = held.tile([P, 2 * rows], F32, name="bias_cols")
             nc.vector.tensor_copy(bias_cols[:], bias_ps[:])
@@ -70,10 +70,10 @@ def tile_mem2seq_kernel(tc, base, x, h, w_ih, w_hh, b_ih, b_hh, offs, out):
             nc.vector.tensor_scalar_mul(neg_b_z[:], b_rz[:, BLOCKS : 2 * BLOCKS], -1.0)
 
             def new_accumulators():
-                ps_r = psum.tile([P, N], F32, name="ps_r", bufs=2)
-                ps_z = psum.tile([P, N], F32, name="ps_z", bufs=2)
+                ps_r = psum.tile([P, N], F32, name="ps_r")
+                ps_z = psum.tile([P, N], F32, name="ps_z")
                 ps_in = psum.tile([P, N], F32, name="ps_in")
-                ps_hn = psum.tile([P, N], F32, name="ps_hn", bufs=2)
+                ps_hn = psum.tile([P, N], F32, name="ps_hn")
                 return {"r": ps_r, "z": ps_z, "in": ps_in, "hn": ps_hn}
 
             def multiply(acc, name, gate, cb, kb, start, stop):
@@ -114,18 +114,21 @@ def tile_mem2seq_kernel(tc, base, x, h, w_ih, w_hh, b_ih, b_hh, offs, out):
                 nc.sync.dma_start(out[cb * P : (cb + 1) * P, :], windows[cb][:])
 
             last = BLOCKS - 1
-            for cb in range(BLOCKS):
-                acc = new_accumulators()
-                for kb in range(BLOCKS):
-                    multiply(acc["r"], "ih", R, cb, kb, start=(kb == 0), stop=False)
-                for kb in range(BLOCKS):
-                    multiply(acc["r"], "hh", R, cb, kb, start=False, stop=(kb == last))
-                for kb in range(BLOCKS):
-                    multiply(acc["hn"], "hh", CAND, cb, kb, start=(kb == 0), stop=(kb == last))
-                for kb in range(BLOCKS):
-                    multiply(acc["z"], "ih", Z, cb, kb, start=(kb == 0), stop=False)
-                for kb in range(BLOCKS):
-                    multiply(acc["z"], "hh", Z, cb, kb, start=False, stop=(kb == last))
-                for kb in range(BLOCKS):
-                    multiply(acc["in"], "ih", CAND, cb, kb, start=(kb == 0), stop=(kb == last))
-                finish_block(cb, acc)
+            for pair in range(BLOCKS // 2):
+                blocks = (2 * pair, 2 * pair + 1)
+                accs = {cb: new_accumulators() for cb in blocks}
+                for name, gate, key, opens, closes in (
+                    ("ih", R, "r", True, False),
+                    ("hh", R, "r", False, True),
+                    ("hh", CAND, "hn", True, True),
+                    ("ih", Z, "z", True, False),
+                    ("hh", Z, "z", False, True),
+                    ("ih", CAND, "in", True, True),
+                ):
+                    for cb in blocks:
+                        for kb in range(BLOCKS):
+                            multiply(
+                                accs[cb][key], name, gate, cb, kb, start=(opens and kb == 0), stop=(closes and kb == last)
+                            )
+                for cb in blocks:
+                    finish_block(cb, accs[cb])

@@ -99,17 +99,14 @@ def tile_mem2seq_kernel(tc, base, x, h, w_ih, w_hh, b_ih, b_hh, offs, out):
                 cand = work.tile([P, N], F32, name="cand")
                 kept = work.tile([P, N], F32, name="kept")
                 fresh = work.tile([P, N], F32, name="fresh")
-                for cols in (slice(0, N // 2), slice(N // 2, N)):
-                    nc.scalar.activation(r[:, cols], acc["r"][:, cols], SIGMOID, bias=b_r)
-                    nc.vector.scalar_tensor_tensor(r_hn[:, cols], acc["hn"][:, cols], b_hn, r[:, cols], op0=ADD, op1=MULT)
-                    nc.scalar.activation(z[:, cols], acc["z"][:, cols], SIGMOID, bias=b_z)
-                    nc.scalar.activation(
-                        one_minus_z[:, cols], acc["z"][:, cols], SIGMOID, bias=neg_b_z[:, cb : cb + 1], scale=-1.0
-                    )
-                    nc.vector.tensor_tensor(kept[:, cols], z[:, cols], moving["hh"][:, cb, cols], MULT)
-                    nc.vector.tensor_tensor(pre_cand[:, cols], r_hn[:, cols], acc["in"][:, cols], ADD)
-                    nc.scalar.activation(cand[:, cols], pre_cand[:, cols], TANH, bias=b_in)
-                    nc.vector.tensor_tensor(fresh[:, cols], one_minus_z[:, cols], cand[:, cols], MULT)
+                nc.scalar.activation(r[:], acc["r"][:], SIGMOID, bias=b_r)
+                nc.vector.scalar_tensor_tensor(r_hn[:], acc["hn"][:], b_hn, r[:], op0=ADD, op1=MULT)
+                nc.scalar.activation(z[:], acc["z"][:], SIGMOID, bias=b_z)
+                nc.scalar.activation(one_minus_z[:], acc["z"][:], SIGMOID, bias=neg_b_z[:, cb : cb + 1], scale=-1.0)
+                nc.vector.tensor_tensor(kept[:], z[:], moving["hh"][:, cb, :], MULT)
+                nc.vector.tensor_tensor(pre_cand[:], r_hn[:], acc["in"][:], ADD)
+                nc.scalar.activation(cand[:], pre_cand[:], TANH, bias=b_in)
+                nc.vector.tensor_tensor(fresh[:], one_minus_z[:], cand[:], MULT)
                 nc.vector.tensor_tensor(windows[cb][:].indirect(offsets[:]), fresh[:], kept[:], ADD)
                 nc.sync.dma_start(out[cb * P : (cb + 1) * P, :], windows[cb][:])
 

@@ -28,30 +28,40 @@ def tile_mem2seq_kernel(tc, base, x, h, w_ih, w_hh, b_ih, b_hh, offs, out):
         tc.tile_pool(name="held", bufs=1) as held,
         tc.tile_pool(name="work", bufs=2) as work,
     ):
-        moving_dram = {"ih": x, "hh": h}
-        w_dram = {"ih": w_ih, "hh": w_hh}
-        moving = {}
-        weights = {}
-        offsets = held.tile([P, N // 16], U16, name="offsets")
+        zeros = held.tile([P, 1], F32, name="zeros")
+        nc.vector.memset(zeros[:], 0.0)
+        table_asked = held.tile([P, 1], F32, name="table_asked")
+        nc.scalar.activation(table_asked[:], zeros[:], SIGMOID)
+
         rows = GATES * BLOCKS
         bias_rows = held.tile([2 * rows, P], F32, name="bias_rows")
+        h_rows = []
+        w_hh_rows = []
+        for kb in range(BLOCKS):
+            h_rows.append(held.tile([P, N], BF16, name=f"h_rows_{kb}"))
+            nc.sync.dma_start(h_rows[kb][:], h[kb * P : (kb + 1) * P, :])
+            w_hh_rows.append(held.tile([P, GATES * C], BF16, name=f"w_hh_rows_{kb}"))
+            if kb == 0:
+                nc.sync.dma_start(w_hh_rows[kb][:, 0:C], w_hh[kb * P : (kb + 1) * P, 0:C])
+                nc.sync.dma_start(w_hh_rows[kb][:, C : GATES * C], w_hh[kb * P : (kb + 1) * P, C : GATES * C])
+            else:
+                nc.sync.dma_start(w_hh_rows[kb][:], w_hh[kb * P : (kb + 1) * P, :])
+        for b_dram, at in ((b_ih, 0), (b_hh, rows)):
+            b_rows = b_dram.rearrange("(g p) o -> g (p o)", p=P)
+            nc.sync.dma_start(bias_rows[at : at + 8, :], b_rows[0:8, :])
+            nc.sync.dma_start(bias_rows[at + 8 : at + rows, :], b_rows[8:rows, :])
+        x_all = held.tile([P, BLOCKS, N], BF16, name="x_all")
+        nc.sync.dma_start(x_all[:], x.rearrange("(kb p) n -> p kb n", p=P))
+        w_ih_cols = {}
+        offsets = held.tile([P, N // 16], U16, name="offsets")
         windows = [held.tile([P, S], F32, name=f"window_{cb}") for cb in range(BLOCKS)]
         for pair in range(BLOCKS // 2):
-            for name, gate in (("ih", R), ("hh", R), ("hh", CAND), ("ih", Z), ("hh", Z), ("ih", CAND)):
-                if name not in moving:
-                    moving[name] = held.tile([P, BLOCKS, N], BF16, name=f"moving_{name}")
-                    nc.sync.dma_start(moving[name][:], moving_dram[name].rearrange("(kb p) n -> p kb n", p=P))
-                w_slice = held.tile([P, BLOCKS, 2 * P], BF16, name=f"w_{name}_{gate}_{pair}")
+            for gate in (R, Z, CAND):
+                w_ih_cols[gate, pair] = held.tile([P, BLOCKS, 2 * P], BF16, name=f"w_ih_cols_{gate}_{pair}")
                 first = gate * C + pair * 2 * P
                 nc.sync.dma_start(
-                    w_slice[:], w_dram[name][:, first : first + 2 * P].rearrange("(kb p) m -> p kb m", p=P)
+                    w_ih_cols[gate, pair][:], w_ih[:, first : first + 2 * P].rearrange("(kb p) m -> p kb m", p=P)
                 )
-                weights[name, gate, pair] = w_slice
-                if (pair, name, gate) == (0, "ih", R):
-                    for b_dram, at in ((b_ih, 0), (b_hh, rows)):
-                        b_rows = b_dram.rearrange("(g p) o -> g (p o)", p=P)
-                        nc.sync.dma_start(bias_rows[at : at + 8, :], b_rows[0:8, :])
-                        nc.sync.dma_start(bias_rows[at + 8 : at + rows, :], b_rows[8:rows, :])
             if pair == 0:
                 nc.sync.dma_start(offsets[:], offs)
             for cb in (2 * pair, 2 * pair + 1):
@@ -74,19 +84,31 @@ def tile_mem2seq_kernel(tc, base, x, h, w_ih, w_hh, b_ih, b_hh, offs, out):
                 ps_z = psum.tile([P, N], F32, name="ps_z")
                 ps_in = psum.tile([P, N], F32, name="ps_in")
                 ps_hn = psum.tile([P, N], F32, name="ps_hn")
-                return {"r": ps_r, "z": ps_z, "in": ps_in, "hn": ps_hn}
+                return {R: ps_r, Z: ps_z, "in": ps_in, "hn": ps_hn}
 
-            def multiply(acc, name, gate, cb, kb, start, stop):
-                half = cb % 2
+            last = BLOCKS - 1
+
+            def multiply_h(acc, gate, cb, kb):
+                first = gate * C + cb * P
                 nc.tensor.matmul(
-                    acc[:],
-                    weights[name, gate, cb // 2][:, kb, half * P : (half + 1) * P],
-                    moving[name][:, kb, :],
-                    start=start,
-                    stop=stop,
+                    acc["hn" if gate == CAND else gate][:],
+                    w_hh_rows[kb][:, first : first + P],
+                    h_rows[kb][:],
+                    start=(kb == 0),
+                    stop=(gate == CAND and kb == last),
                 )
 
-            def finish_block(cb, acc):
+            def multiply_x(acc, gate, cb, kb):
+                half = cb % 2
+                nc.tensor.matmul(
+                    acc["in" if gate == CAND else gate][:],
+                    w_ih_cols[gate, cb // 2][:, kb, half * P : (half + 1) * P],
+                    x_all[:, kb, :],
+                    start=(gate == CAND and kb == 0),
+                    stop=(kb == last),
+                )
+
+            def factors(cb, acc):
                 b_r = b_rz[:, cb : cb + 1]
                 b_z = b_rz[:, BLOCKS + cb : BLOCKS + cb + 1]
                 b_in = bias_cols[:, CAND * BLOCKS + cb : CAND * BLOCKS + cb + 1]
@@ -98,34 +120,31 @@ def tile_mem2seq_kernel(tc, base, x, h, w_ih, w_hh, b_ih, b_hh, offs, out):
                 pre_cand = work.tile([P, N], F32, name="pre_cand")
                 cand = work.tile([P, N], F32, name="cand")
                 kept = work.tile([P, N], F32, name="kept")
-                fresh = work.tile([P, N], F32, name="fresh")
-                nc.scalar.activation(r[:], acc["r"][:], SIGMOID, bias=b_r)
+                nc.scalar.activation(r[:], acc[R][:], SIGMOID, bias=b_r)
                 nc.vector.scalar_tensor_tensor(r_hn[:], acc["hn"][:], b_hn, r[:], op0=ADD, op1=MULT)
-                nc.scalar.activation(z[:], acc["z"][:], SIGMOID, bias=b_z)
-                nc.scalar.activation(one_minus_z[:], acc["z"][:], SIGMOID, bias=neg_b_z[:, cb : cb + 1], scale=-1.0)
-                nc.vector.tensor_tensor(kept[:], z[:], moving["hh"][:, cb, :], MULT)
+                nc.scalar.activation(z[:], acc[Z][:], SIGMOID, bias=b_z)
+                nc.scalar.activation(one_minus_z[:], acc[Z][:], SIGMOID, bias=neg_b_z[:, cb : cb + 1], scale=-1.0)
+                nc.vector.tensor_tensor(kept[:], z[:], h_rows[cb][:], MULT)
                 nc.vector.tensor_tensor(pre_cand[:], r_hn[:], acc["in"][:], ADD)
                 nc.scalar.activation(cand[:], pre_cand[:], TANH, bias=b_in)
+                return one_minus_z, cand, kept
+
+            def place(cb, one_minus_z, cand, kept):
+                fresh = work.tile([P, N], F32, name="fresh")
                 nc.vector.tensor_tensor(fresh[:], one_minus_z[:], cand[:], MULT)
                 nc.vector.tensor_tensor(windows[cb][:].indirect(offsets[:]), fresh[:], kept[:], ADD)
                 nc.sync.dma_start(out[cb * P : (cb + 1) * P, :], windows[cb][:])
 
-            last = BLOCKS - 1
             for pair in range(BLOCKS // 2):
                 blocks = (2 * pair, 2 * pair + 1)
                 accs = {cb: new_accumulators() for cb in blocks}
-                for name, gate, key, opens, closes in (
-                    ("ih", R, "r", True, False),
-                    ("hh", R, "r", False, True),
-                    ("hh", CAND, "hn", True, True),
-                    ("ih", Z, "z", True, False),
-                    ("hh", Z, "z", False, True),
-                    ("ih", CAND, "in", True, True),
-                ):
+                for kb in range(BLOCKS):
+                    for gate in (R, CAND, Z):
+                        for cb in blocks:
+                            multiply_h(accs[cb], gate, cb, kb)
+                for gate in (R, Z, CAND):
                     for cb in blocks:
                         for kb in range(BLOCKS):
-                            multiply(
-                                accs[cb][key], name, gate, cb, kb, start=(opens and kb == 0), stop=(closes and kb == last)
-                            )
+                            multiply_x(accs[cb], gate, cb, kb)
                 for cb in blocks:
-                    finish_block(cb, accs[cb])
+                    place(cb, *factors(cb, accs[cb]))

@@ -33,35 +33,49 @@ def tile_mem2seq_kernel(tc, base, x, h, w_ih, w_hh, b_ih, b_hh, offs, out):
         table_asked = held.tile([P, 1], F32, name="table_asked")
         nc.scalar.activation(table_asked[:], zeros[:], SIGMOID)
 
+        pieces = {
+            0: (("h", 0), ("h", 1), ("x", R), ("h", 2), ("x", Z), ("h", 3), ("x", CAND)),
+            1: (("h", 0), ("h", 1), ("h", 2), ("h", 3), ("x", R), ("x", Z), ("x", CAND)),
+        }
+        h_rows = {}
+        w_hh_rows = {}
+        x_all = held.tile([P, BLOCKS, N], BF16, name="x_all")
+        w_ih_cols = {}
         rows = GATES * BLOCKS
         bias_rows = held.tile([2 * rows, P], F32, name="bias_rows")
-        h_rows = []
-        w_hh_rows = []
-        for kb in range(BLOCKS):
-            h_rows.append(held.tile([P, N], BF16, name=f"h_rows_{kb}"))
+        offsets = held.tile([P, N // 16], U16, name="offsets")
+        windows = [held.tile([P, S], F32, name=f"window_{cb}") for cb in range(BLOCKS)]
+
+        def load_h_piece(kb):
+            h_rows[kb] = held.tile([P, N], BF16, name=f"h_rows_{kb}")
             nc.sync.dma_start(h_rows[kb][:], h[kb * P : (kb + 1) * P, :])
-            w_hh_rows.append(held.tile([P, GATES * C], BF16, name=f"w_hh_rows_{kb}"))
+            w_hh_rows[kb] = held.tile([P, GATES * C], BF16, name=f"w_hh_rows_{kb}")
             if kb == 0:
                 nc.sync.dma_start(w_hh_rows[kb][:, 0:C], w_hh[kb * P : (kb + 1) * P, 0:C])
                 nc.sync.dma_start(w_hh_rows[kb][:, C : GATES * C], w_hh[kb * P : (kb + 1) * P, C : GATES * C])
             else:
                 nc.sync.dma_start(w_hh_rows[kb][:], w_hh[kb * P : (kb + 1) * P, :])
-        for b_dram, at in ((b_ih, 0), (b_hh, rows)):
-            b_rows = b_dram.rearrange("(g p) o -> g (p o)", p=P)
-            nc.sync.dma_start(bias_rows[at : at + 8, :], b_rows[0:8, :])
-            nc.sync.dma_start(bias_rows[at + 8 : at + rows, :], b_rows[8:rows, :])
-        x_all = held.tile([P, BLOCKS, N], BF16, name="x_all")
-        nc.sync.dma_start(x_all[:], x.rearrange("(kb p) n -> p kb n", p=P))
-        w_ih_cols = {}
-        offsets = held.tile([P, N // 16], U16, name="offsets")
-        windows = [held.tile([P, S], F32, name=f"window_{cb}") for cb in range(BLOCKS)]
+
+        def load_x_piece(gate, pair):
+            w_ih_cols[gate, pair] = held.tile([P, BLOCKS, 2 * P], BF16, name=f"w_ih_cols_{gate}_{pair}")
+            at = gate * C + pair * 2 * P
+            nc.sync.dma_start(
+                w_ih_cols[gate, pair][:], w_ih[:, at : at + 2 * P].rearrange("(p kb) m -> p kb m", kb=BLOCKS)
+            )
+
         for pair in range(BLOCKS // 2):
-            for gate in (R, Z, CAND):
-                w_ih_cols[gate, pair] = held.tile([P, BLOCKS, 2 * P], BF16, name=f"w_ih_cols_{gate}_{pair}")
-                first = gate * C + pair * 2 * P
-                nc.sync.dma_start(
-                    w_ih_cols[gate, pair][:], w_ih[:, first : first + 2 * P].rearrange("(kb p) m -> p kb m", p=P)
-                )
+            for source, which in pieces[pair]:
+                if source == "h" and pair == 0:
+                    load_h_piece(which)
+                if source == "x":
+                    if (pair, which) == (0, R):
+                        nc.sync.dma_start(x_all[:], x.rearrange("(p kb) n -> p kb n", kb=BLOCKS))
+                    load_x_piece(which, pair)
+                    if (pair, which) == (0, R):
+                        for b_dram, at in ((b_ih, 0), (b_hh, rows)):
+                            b_rows = b_dram.rearrange("(g p) o -> g (p o)", p=P)
+                            nc.sync.dma_start(bias_rows[at : at + 8, :], b_rows[0:8, :])
+                            nc.sync.dma_start(bias_rows[at + 8 : at + rows, :], b_rows[8:rows, :])
             if pair == 0:
                 nc.sync.dma_start(offsets[:], offs)
             for cb in (2 * pair, 2 * pair + 1):
@@ -84,31 +98,38 @@ def tile_mem2seq_kernel(tc, base, x, h, w_ih, w_hh, b_ih, b_hh, offs, out):
                 ps_z = psum.tile([P, N], F32, name="ps_z")
                 ps_in = psum.tile([P, N], F32, name="ps_in")
                 ps_hn = psum.tile([P, N], F32, name="ps_hn")
-                return {R: ps_r, Z: ps_z, "in": ps_in, "hn": ps_hn}
+                return {"r": ps_r, "z": ps_z, "in": ps_in, "hn": ps_hn}
 
-            last = BLOCKS - 1
+            def sum_of(source, gate):
+                if gate == CAND:
+                    return "hn" if source == "h" else "in"
+                return "r" if gate == R else "z"
 
-            def multiply_h(acc, gate, cb, kb):
-                first = gate * C + cb * P
-                nc.tensor.matmul(
-                    acc["hn" if gate == CAND else gate][:],
-                    w_hh_rows[kb][:, first : first + P],
-                    h_rows[kb][:],
-                    start=(kb == 0),
-                    stop=(gate == CAND and kb == last),
-                )
+            def multiply_pair(pair, accs):
+                blocks = (2 * pair, 2 * pair + 1)
+                todo = []
+                for source, which in pieces[pair]:
+                    if source == "h":
+                        todo.extend(("h", gate, cb, which) for gate in (R, CAND, Z) for cb in blocks)
+                    else:
+                        todo.extend(("x", which, cb, kb) for cb in blocks for kb in range(BLOCKS))
+                sums = [(cb, sum_of(source, gate)) for source, gate, cb, kb in todo]
+                for i, (source, gate, cb, kb) in enumerate(todo):
+                    if source == "h":
+                        at = gate * C + cb * P
+                        stationary, moving = w_hh_rows[kb][:, at : at + P], h_rows[kb][:]
+                    else:
+                        at = (cb % 2) * P
+                        stationary, moving = w_ih_cols[gate, pair][:, kb, at : at + P], x_all[:, kb, :]
+                    nc.tensor.matmul(
+                        accs[cb][sum_of(source, gate)][:],
+                        stationary,
+                        moving,
+                        start=(sums[i] not in sums[:i]),
+                        stop=(sums[i] not in sums[i + 1 :]),
+                    )
 
-            def multiply_x(acc, gate, cb, kb):
-                half = cb % 2
-                nc.tensor.matmul(
-                    acc["in" if gate == CAND else gate][:],
-                    w_ih_cols[gate, cb // 2][:, kb, half * P : (half + 1) * P],
-                    x_all[:, kb, :],
-                    start=(gate == CAND and kb == 0),
-                    stop=(kb == last),
-                )
-
-            def factors(cb, acc):
+            def finish_block(cb, acc):
                 b_r = b_rz[:, cb : cb + 1]
                 b_z = b_rz[:, BLOCKS + cb : BLOCKS + cb + 1]
                 b_in = bias_cols[:, CAND * BLOCKS + cb : CAND * BLOCKS + cb + 1]
@@ -120,31 +141,20 @@ def tile_mem2seq_kernel(tc, base, x, h, w_ih, w_hh, b_ih, b_hh, offs, out):
                 pre_cand = work.tile([P, N], F32, name="pre_cand")
                 cand = work.tile([P, N], F32, name="cand")
                 kept = work.tile([P, N], F32, name="kept")
-                nc.scalar.activation(r[:], acc[R][:], SIGMOID, bias=b_r)
+                fresh = work.tile([P, N], F32, name="fresh")
+                nc.scalar.activation(r[:], acc["r"][:], SIGMOID, bias=b_r)
                 nc.vector.scalar_tensor_tensor(r_hn[:], acc["hn"][:], b_hn, r[:], op0=ADD, op1=MULT)
-                nc.scalar.activation(z[:], acc[Z][:], SIGMOID, bias=b_z)
-                nc.scalar.activation(one_minus_z[:], acc[Z][:], SIGMOID, bias=neg_b_z[:, cb : cb + 1], scale=-1.0)
+                nc.scalar.activation(z[:], acc["z"][:], SIGMOID, bias=b_z)
+                nc.scalar.activation(one_minus_z[:], acc["z"][:], SIGMOID, bias=neg_b_z[:, cb : cb + 1], scale=-1.0)
                 nc.vector.tensor_tensor(kept[:], z[:], h_rows[cb][:], MULT)
                 nc.vector.tensor_tensor(pre_cand[:], r_hn[:], acc["in"][:], ADD)
                 nc.scalar.activation(cand[:], pre_cand[:], TANH, bias=b_in)
-                return one_minus_z, cand, kept
-
-            def place(cb, one_minus_z, cand, kept):
-                fresh = work.tile([P, N], F32, name="fresh")
                 nc.vector.tensor_tensor(fresh[:], one_minus_z[:], cand[:], MULT)
                 nc.vector.tensor_tensor(windows[cb][:].indirect(offsets[:]), fresh[:], kept[:], ADD)
                 nc.sync.dma_start(out[cb * P : (cb + 1) * P, :], windows[cb][:])
 
             for pair in range(BLOCKS // 2):
-                blocks = (2 * pair, 2 * pair + 1)
-                accs = {cb: new_accumulators() for cb in blocks}
-                for kb in range(BLOCKS):
-                    for gate in (R, CAND, Z):
-                        for cb in blocks:
-                            multiply_h(accs[cb], gate, cb, kb)
-                for gate in (R, Z, CAND):
-                    for cb in blocks:
-                        for kb in range(BLOCKS):
-                            multiply_x(accs[cb], gate, cb, kb)
-                for cb in blocks:
-                    place(cb, *factors(cb, accs[cb]))
+                accs = {cb: new_accumulators() for cb in (2 * pair, 2 * pair + 1)}
+                multiply_pair(pair, accs)
+                for cb in (2 * pair, 2 * pair + 1):
+                    finish_block(cb, accs[cb])

@@ -33,9 +33,10 @@ def tile_mem2seq_kernel(tc, base, x, h, w_ih, w_hh, b_ih, b_hh, offs, out):
         table_asked = held.tile([P, 1], F32, name="table_asked")
         nc.scalar.activation(table_asked[:], zeros[:], SIGMOID)
 
+        every = tuple(range(BLOCKS))
         pieces = {
-            0: (("h", 0), ("h", 1), ("x", R), ("h", 2), ("x", Z), ("h", 3), ("x", CAND)),
-            1: (("h", 0), ("h", 1), ("h", 2), ("h", 3), ("x", R), ("x", Z), ("x", CAND)),
+            0: (("h", 0), ("h", 1), ("x", R, every), ("h", 2), ("x", Z, every), ("h", 3), ("x", CAND, (0, 1)), ("x", CAND, (2, 3))),
+            1: (("h", 0), ("h", 1), ("h", 2), ("h", 3), ("x", R, every), ("x", Z, every), ("x", CAND, every)),
         }
         h_rows = {}
         w_hh_rows = {}
@@ -56,26 +57,26 @@ def tile_mem2seq_kernel(tc, base, x, h, w_ih, w_hh, b_ih, b_hh, offs, out):
             else:
                 nc.sync.dma_start(w_hh_rows[kb][:], w_hh[kb * P : (kb + 1) * P, :])
 
-        def load_x_piece(gate, pair):
-            w_ih_cols[gate, pair] = held.tile([P, BLOCKS, 2 * P], BF16, name=f"w_ih_cols_{gate}_{pair}")
+        def load_x_piece(gate, kbs, pair):
+            if (gate, pair) not in w_ih_cols:
+                w_ih_cols[gate, pair] = held.tile([P, BLOCKS, 2 * P], BF16, name=f"w_ih_cols_{gate}_{pair}")
             at = gate * C + pair * 2 * P
-            nc.sync.dma_start(
-                w_ih_cols[gate, pair][:], w_ih[:, at : at + 2 * P].rearrange("(p kb) m -> p kb m", kb=BLOCKS)
-            )
+            columns = w_ih[:, at : at + 2 * P].rearrange("(p kb) m -> p kb m", kb=BLOCKS)
+            nc.sync.dma_start(w_ih_cols[gate, pair][:, kbs[0] : kbs[-1] + 1, :], columns[:, kbs[0] : kbs[-1] + 1, :])
+
+        for b_dram, at in ((b_ih, 0), (b_hh, rows)):
+            b_rows = b_dram.rearrange("(g p) o -> g (p o)", p=P)
+            nc.scalar.dma_start(bias_rows[at : at + 8, :], b_rows[0:8, :])
+            nc.scalar.dma_start(bias_rows[at + 8 : at + rows, :], b_rows[8:rows, :])
 
         for pair in range(BLOCKS // 2):
-            for source, which in pieces[pair]:
-                if source == "h" and pair == 0:
-                    load_h_piece(which)
-                if source == "x":
-                    if (pair, which) == (0, R):
+            for piece in pieces[pair]:
+                if piece[0] == "h" and pair == 0:
+                    load_h_piece(piece[1])
+                if piece[0] == "x":
+                    if (pair, piece[1]) == (0, R):
                         nc.sync.dma_start(x_all[:], x.rearrange("(p kb) n -> p kb n", kb=BLOCKS))
-                    load_x_piece(which, pair)
-                    if (pair, which) == (0, R):
-                        for b_dram, at in ((b_ih, 0), (b_hh, rows)):
-                            b_rows = b_dram.rearrange("(g p) o -> g (p o)", p=P)
-                            nc.sync.dma_start(bias_rows[at : at + 8, :], b_rows[0:8, :])
-                            nc.sync.dma_start(bias_rows[at + 8 : at + rows, :], b_rows[8:rows, :])
+                    load_x_piece(piece[1], piece[2], pair)
             if pair == 0:
                 nc.sync.dma_start(offsets[:], offs)
             for cb in (2 * pair, 2 * pair + 1):
@@ -108,11 +109,11 @@ def tile_mem2seq_kernel(tc, base, x, h, w_ih, w_hh, b_ih, b_hh, offs, out):
             def multiply_pair(pair, accs):
                 blocks = (2 * pair, 2 * pair + 1)
                 todo = []
-                for source, which in pieces[pair]:
-                    if source == "h":
-                        todo.extend(("h", gate, cb, which) for gate in (R, CAND, Z) for cb in blocks)
+                for piece in pieces[pair]:
+                    if piece[0] == "h":
+                        todo.extend(("h", gate, cb, piece[1]) for gate in (R, CAND, Z) for cb in blocks)
                     else:
-                        todo.extend(("x", which, cb, kb) for cb in blocks for kb in range(BLOCKS))
+                        todo.extend(("x", piece[1], cb, kb) for cb in blocks for kb in piece[2])
                 sums = [(cb, sum_of(source, gate)) for source, gate, cb, kb in todo]
                 for i, (source, gate, cb, kb) in enumerate(todo):
                     if source == "h":

@@ -36,7 +36,7 @@ def tile_mem2seq_kernel(tc, base, x, h, w_ih, w_hh, b_ih, b_hh, offs, out):
         every = tuple(range(BLOCKS))
         pieces = {
             0: (("h", 0), ("h", 1), ("x", R, every), ("h", 2), ("x", Z, every), ("h", 3), ("x", CAND, (0, 1)), ("x", CAND, (2, 3))),
-            1: (("h", 0), ("h", 1), ("h", 2), ("h", 3), ("x", R, every), ("x", Z, every), ("x", CAND, every)),
+            1: (("all h",), ("x", R, every), ("x", Z, every), ("x", CAND, every)),
         }
         h_rows = {}
         w_hh_rows = {}
@@ -112,6 +112,8 @@ def tile_mem2seq_kernel(tc, base, x, h, w_ih, w_hh, b_ih, b_hh, offs, out):
                 for piece in pieces[pair]:
                     if piece[0] == "h":
                         todo.extend(("h", gate, cb, piece[1]) for gate in (R, CAND, Z) for cb in blocks)
+                    elif piece[0] == "all h":
+                        todo.extend(("h", gate, cb, kb) for gate in (R, CAND, Z) for cb in blocks for kb in every)
                     else:
                         todo.extend(("x", piece[1], cb, kb) for cb in blocks for kb in piece[2])
                 sums = [(cb, sum_of(source, gate)) for source, gate, cb, kb in todo]

@@ -150,9 +150,12 @@ def tile_mem2seq_kernel(tc, base, x, h, w_ih, w_hh, b_ih, b_hh, offs, out):
                 nc.scalar.activation(z[:], acc["z"][:], SIGMOID, bias=b_z)
                 nc.scalar.activation(one_minus_z[:], acc["z"][:], SIGMOID, bias=neg_b_z[:, cb : cb + 1], scale=-1.0)
                 nc.vector.tensor_tensor(kept[:], z[:], h_rows[cb][:], MULT)
-                nc.vector.tensor_tensor(pre_cand[:], r_hn[:], acc["in"][:], ADD)
-                nc.scalar.activation(cand[:], pre_cand[:], TANH, bias=b_in)
-                nc.vector.tensor_tensor(fresh[:], one_minus_z[:], cand[:], MULT)
+                halves = (slice(0, N // 2), slice(N // 2, N))
+                for half in halves:
+                    nc.vector.tensor_tensor(pre_cand[:, half], r_hn[:, half], acc["in"][:, half], ADD)
+                    nc.scalar.activation(cand[:, half], pre_cand[:, half], TANH, bias=b_in)
+                for half in halves:
+                    nc.vector.tensor_tensor(fresh[:, half], one_minus_z[:, half], cand[:, half], MULT)
                 nc.vector.tensor_tensor(windows[cb][:].indirect(offsets[:]), fresh[:], kept[:], ADD)
                 nc.sync.dma_start(out[cb * P : (cb + 1) * P, :], windows[cb][:])
 

@@ -6,6 +6,7 @@ BF16 = mybir.dt.bfloat16
 U16 = mybir.dt.uint16
 ADD = mybir.AluOpType.add
 MULT = mybir.AluOpType.mult
+SUBTRACT = mybir.AluOpType.subtract
 SIGMOID = mybir.ActivationFunctionType.Sigmoid
 TANH = mybir.ActivationFunctionType.Tanh
 
@@ -38,7 +39,8 @@ def tile_mem2seq_kernel(tc, base, x, h, w_ih, w_hh, b_ih, b_hh, offs, out):
             0: (("h", 0), ("h", 1), ("x", R, every), ("h", 2), ("x", Z, every), ("h", 3), ("x", CAND, (0, 1)), ("x", CAND, (2, 3))),
             1: (("all h",), ("x", R, every), ("x", Z, every), ("x", CAND, every)),
         }
-        h_rows = {}
+        h_all = held.tile([P, BLOCKS, N], BF16, name="h_all")
+        h_blocks = h.rearrange("(kb p) n -> p kb n", p=P)
         w_hh_rows = {}
         x_all = held.tile([P, BLOCKS, N], BF16, name="x_all")
         w_ih_cols = {}
@@ -48,12 +50,13 @@ def tile_mem2seq_kernel(tc, base, x, h, w_ih, w_hh, b_ih, b_hh, offs, out):
         windows = [held.tile([P, S], F32, name=f"window_{cb}") for cb in range(BLOCKS)]
 
         def load_h_piece(kb):
-            h_rows[kb] = held.tile([P, N], BF16, name=f"h_rows_{kb}")
-            nc.sync.dma_start(h_rows[kb][:], h[kb * P : (kb + 1) * P, :])
+            if kb == 0:
+                nc.sync.dma_start(h_all[:, 0, :], h_blocks[:, 0, :])
             w_hh_rows[kb] = held.tile([P, GATES * C], BF16, name=f"w_hh_rows_{kb}")
             if kb == 0:
                 nc.sync.dma_start(w_hh_rows[kb][:, 0:C], w_hh[kb * P : (kb + 1) * P, 0:C])
                 nc.sync.dma_start(w_hh_rows[kb][:, C : GATES * C], w_hh[kb * P : (kb + 1) * P, C : GATES * C])
+                nc.sync.dma_start(h_all[:, 1:BLOCKS, :], h_blocks[:, 1:BLOCKS, :])
             else:
                 nc.sync.dma_start(w_hh_rows[kb][:], w_hh[kb * P : (kb + 1) * P, :])
 
@@ -64,15 +67,18 @@ def tile_mem2seq_kernel(tc, base, x, h, w_ih, w_hh, b_ih, b_hh, offs, out):
             columns = w_ih[:, at : at + 2 * P].rearrange("(p kb) m -> p kb m", kb=BLOCKS)
             nc.sync.dma_start(w_ih_cols[gate, pair][:, kbs[0] : kbs[-1] + 1, :], columns[:, kbs[0] : kbs[-1] + 1, :])
 
-        for b_dram, at in ((b_ih, 0), (b_hh, rows)):
-            b_rows = b_dram.rearrange("(g p) o -> g (p o)", p=P)
-            nc.scalar.dma_start(bias_rows[at : at + 8, :], b_rows[0:8, :])
-            nc.scalar.dma_start(bias_rows[at + 8 : at + rows, :], b_rows[8:rows, :])
+        def load_biases():
+            for b_dram, at in ((b_ih, 0), (b_hh, rows)):
+                b_rows = b_dram.rearrange("(g p) o -> g (p o)", p=P)
+                nc.sync.dma_start(bias_rows[at : at + 8, :], b_rows[0:8, :])
+                nc.sync.dma_start(bias_rows[at + 8 : at + rows, :], b_rows[8:rows, :])
 
         for pair in range(BLOCKS // 2):
             for piece in pieces[pair]:
                 if piece[0] == "h" and pair == 0:
                     load_h_piece(piece[1])
+                    if piece[1] == 1:
+                        load_biases()
                 if piece[0] == "x":
                     if (pair, piece[1]) == (0, R):
                         nc.sync.dma_start(x_all[:], x.rearrange("(p kb) n -> p kb n", kb=BLOCKS))
@@ -91,8 +97,8 @@ def tile_mem2seq_kernel(tc, base, x, h, w_ih, w_hh, b_ih, b_hh, offs, out):
             nc.vector.tensor_copy(bias_cols[:], bias_ps[:])
             b_rz = held.tile([P, 2 * BLOCKS], F32, name="b_rz")
             nc.vector.tensor_tensor(b_rz[:], bias_cols[:, 0 : 2 * BLOCKS], bias_cols[:, rows : rows + 2 * BLOCKS], ADD)
-            neg_b_z = held.tile([P, BLOCKS], F32, name="neg_b_z")
-            nc.vector.tensor_scalar_mul(neg_b_z[:], b_rz[:, BLOCKS : 2 * BLOCKS], -1.0)
+            neg_b_in = held.tile([P, BLOCKS], F32, name="neg_b_in")
+            nc.vector.tensor_scalar_mul(neg_b_in[:], bias_cols[:, CAND * BLOCKS : rows], -1.0)
 
             def new_accumulators():
                 ps_r = psum.tile([P, N], F32, name="ps_r")
@@ -120,7 +126,7 @@ def tile_mem2seq_kernel(tc, base, x, h, w_ih, w_hh, b_ih, b_hh, offs, out):
                 for i, (source, gate, cb, kb) in enumerate(todo):
                     if source == "h":
                         at = gate * C + cb * P
-                        stationary, moving = w_hh_rows[kb][:, at : at + P], h_rows[kb][:]
+                        stationary, moving = w_hh_rows[kb][:, at : at + P], h_all[:, kb, :]
                     else:
                         at = (cb % 2) * P
                         stationary, moving = w_ih_cols[gate, pair][:, kb, at : at + P], x_all[:, kb, :]
@@ -135,27 +141,24 @@ def tile_mem2seq_kernel(tc, base, x, h, w_ih, w_hh, b_ih, b_hh, offs, out):
             def finish_block(cb, acc):
                 b_r = b_rz[:, cb : cb + 1]
                 b_z = b_rz[:, BLOCKS + cb : BLOCKS + cb + 1]
-                b_in = bias_cols[:, CAND * BLOCKS + cb : CAND * BLOCKS + cb + 1]
                 b_hn = bias_cols[:, rows + CAND * BLOCKS + cb : rows + CAND * BLOCKS + cb + 1]
                 r = work.tile([P, N], F32, name="r")
                 z = work.tile([P, N], F32, name="z")
-                one_minus_z = work.tile([P, N], F32, name="one_minus_z")
                 r_hn = work.tile([P, N], F32, name="r_hn")
                 pre_cand = work.tile([P, N], F32, name="pre_cand")
-                cand = work.tile([P, N], F32, name="cand")
+                neg_cand = work.tile([P, N], F32, name="neg_cand")
                 kept = work.tile([P, N], F32, name="kept")
                 fresh = work.tile([P, N], F32, name="fresh")
                 nc.scalar.activation(r[:], acc["r"][:], SIGMOID, bias=b_r)
                 nc.vector.scalar_tensor_tensor(r_hn[:], acc["hn"][:], b_hn, r[:], op0=ADD, op1=MULT)
                 nc.scalar.activation(z[:], acc["z"][:], SIGMOID, bias=b_z)
-                nc.scalar.activation(one_minus_z[:], acc["z"][:], SIGMOID, bias=neg_b_z[:, cb : cb + 1], scale=-1.0)
-                nc.vector.tensor_tensor(kept[:], z[:], h_rows[cb][:], MULT)
+                nc.vector.tensor_tensor(kept[:], z[:], h_all[:, cb, :], MULT)
                 halves = (slice(0, N // 2), slice(N // 2, N))
                 for half in halves:
                     nc.vector.tensor_tensor(pre_cand[:, half], r_hn[:, half], acc["in"][:, half], ADD)
-                    nc.scalar.activation(cand[:, half], pre_cand[:, half], TANH, bias=b_in)
+                    nc.scalar.activation(neg_cand[:, half], pre_cand[:, half], TANH, bias=neg_b_in[:, cb : cb + 1], scale=-1.0)
                 for half in halves:
-                    nc.vector.tensor_tensor(fresh[:, half], one_minus_z[:, half], cand[:, half], MULT)
+                    nc.vector.scalar_tensor_tensor(fresh[:, half], z[:, half], 1.0, neg_cand[:, half], op0=SUBTRACT, op1=MULT)
                 nc.vector.tensor_tensor(windows[cb][:].indirect(offsets[:]), fresh[:], kept[:], ADD)
                 nc.sync.dma_start(out[cb * P : (cb + 1) * P, :], windows[cb][:])
 

import concourse.mybir as mybir
from concourse.masks import make_identity

F32 = mybir.dt.float32
BF16 = mybir.dt.bfloat16
U16 = mybir.dt.uint16
ADD = mybir.AluOpType.add
MULT = mybir.AluOpType.mult
SUBTRACT = mybir.AluOpType.subtract
SIGMOID = mybir.ActivationFunctionType.Sigmoid
TANH = mybir.ActivationFunctionType.Tanh

P = 128
C = 512
S = 1024
N = 256
BLOCKS = C // P
R = 0
Z = 1
CAND = 2
GATES = 3

FLOPS = 2 * 2 * C * GATES * C * N


def tile_mem2seq_kernel(tc, base, x, h, w_ih, w_hh, b_ih, b_hh, offs, out):
    nc = tc.nc
    with (
        tc.tile_pool(name="held", bufs=1) as held,
        tc.tile_pool(name="work", bufs=2) as work,
    ):
        zeros = held.tile([P, 1], F32, name="zeros")
        nc.vector.memset(zeros[:], 0.0)
        table_asked = held.tile([P, 1], F32, name="table_asked")
        nc.scalar.activation(table_asked[:], zeros[:], SIGMOID)

        every = tuple(range(BLOCKS))
        pieces = {
            0: (("h", 0), ("h", 1), ("x", R, every), ("h", 2), ("x", Z, every), ("h", 3), ("x", CAND, (0, 1)), ("x", CAND, (2, 3))),
            1: (("all h",), ("x", R, every), ("x", Z, every), ("x", CAND, every)),
        }
        h_all = held.tile([P, BLOCKS, N], BF16, name="h_all")
        h_blocks = h.rearrange("(kb p) n -> p kb n", p=P)
        w_hh_rows = {}
        x_all = held.tile([P, BLOCKS, N], BF16, name="x_all")
        w_ih_cols = {}
        rows = GATES * BLOCKS
        bias_rows = held.tile([2 * rows, P], F32, name="bias_rows")
        offsets = held.tile([P, N // 16], U16, name="offsets")
        windows = [held.tile([P, S], F32, name=f"window_{cb}") for cb in range(BLOCKS)]

        def load_h_piece(kb):
            if kb == 0:
                nc.sync.dma_start(h_all[:, 0, :], h_blocks[:, 0, :])
            w_hh_rows[kb] = held.tile([P, GATES * C], BF16, name=f"w_hh_rows_{kb}")
            if kb == 0:
                nc.sync.dma_start(w_hh_rows[kb][:, 0:C], w_hh[kb * P : (kb + 1) * P, 0:C])
                nc.sync.dma_start(w_hh_rows[kb][:, C : GATES * C], w_hh[kb * P : (kb + 1) * P, C : GATES * C])
                nc.sync.dma_start(h_all[:, 1:BLOCKS, :], h_blocks[:, 1:BLOCKS, :])
            else:
                nc.sync.dma_start(w_hh_rows[kb][:], w_hh[kb * P : (kb + 1) * P, :])

        def load_x_piece(gate, kbs, pair):
            if (gate, pair) not in w_ih_cols:
                w_ih_cols[gate, pair] = held.tile([P, BLOCKS, 2 * P], BF16, name=f"w_ih_cols_{gate}_{pair}")
            at = gate * C + pair * 2 * P
            columns = w_ih[:, at : at + 2 * P].rearrange("(p kb) m -> p kb m", kb=BLOCKS)
            nc.sync.dma_start(w_ih_cols[gate, pair][:, kbs[0] : kbs[-1] + 1, :], columns[:, kbs[0] : kbs[-1] + 1, :])

        def load_biases():
            for b_dram, at in ((b_ih, 0), (b_hh, rows)):
                b_rows = b_dram.rearrange("(g p) o -> g (p o)", p=P)
                nc.sync.dma_start(bias_rows[at : at + 8, :], b_rows[0:8, :])
                nc.sync.dma_start(bias_rows[at + 8 : at + rows, :], b_rows[8:rows, :])

        for pair in range(BLOCKS // 2):
            for piece in pieces[pair]:
                if piece[0] == "h" and pair == 0:
                    load_h_piece(piece[1])
                    if piece[1] == 1:
                        load_biases()
                if piece[0] == "x":
                    if (pair, piece[1]) == (0, R):
                        nc.sync.dma_start(x_all[:], x.rearrange("(p kb) n -> p kb n", kb=BLOCKS))
                    load_x_piece(piece[1], piece[2], pair)
            if pair == 0:
                nc.sync.dma_start(offsets[:], offs)
            for cb in (2 * pair, 2 * pair + 1):
                nc.sync.dma_start(windows[cb][:], base[cb * P : (cb + 1) * P, :])

        with tc.psum_pool(name="psum", bufs=2) as psum:
            identity = held.tile([2 * rows, 2 * rows], F32, name="identity")
            make_identity(nc, identity[:])
            bias_ps = psum.tile([P, 2 * rows], F32, name="bias_ps", tag="ps_in")
            nc.tensor.matmul(bias_ps[:], bias_rows[:], identity[:], start=True, stop=True)
            bias_cols = held.tile([P, 2 * rows], F32, name="bias_cols")
            nc.vector.tensor_copy(bias_cols[:], bias_ps[:])
            b_rz = held.tile([P, 2 * BLOCKS], F32, name="b_rz")
            nc.vector.tensor_tensor(b_rz[:], bias_cols[:, 0 : 2 * BLOCKS], bias_cols[:, rows : rows + 2 * BLOCKS], ADD)
            neg_b_in = held.tile([P, BLOCKS], F32, name="neg_b_in")
            nc.vector.tensor_scalar_mul(neg_b_in[:], bias_cols[:, CAND * BLOCKS : rows], -1.0)

            def new_accumulators():
                ps_r = psum.tile([P, N], F32, name="ps_r")
                ps_z = psum.tile([P, N], F32, name="ps_z")
                ps_in = psum.tile([P, N], F32, name="ps_in")
                ps_hn = psum.tile([P, N], F32, name="ps_hn")
                return {"r": ps_r, "z": ps_z, "in": ps_in, "hn": ps_hn}

            def sum_of(source, gate):
                if gate == CAND:
                    return "hn" if source == "h" else "in"
                return "r" if gate == R else "z"

            def multiply_pair(pair, accs):
                blocks = (2 * pair, 2 * pair + 1)
                todo = []
                for piece in pieces[pair]:
                    if piece[0] == "h":
                        todo.extend(("h", gate, cb, piece[1]) for gate in (R, CAND, Z) for cb in blocks)
                    elif piece[0] == "all h":
                        todo.extend(("h", gate, cb, kb) for gate in (R, CAND, Z) for cb in blocks for kb in every)
                    else:
                        todo.extend(("x", piece[1], cb, kb) for cb in blocks for kb in piece[2])
                sums = [(cb, sum_of(source, gate)) for source, gate, cb, kb in todo]
                for i, (source, gate, cb, kb) in enumerate(todo):
                    if source == "h":
                        at = gate * C + cb * P
                        stationary, moving = w_hh_rows[kb][:, at : at + P], h_all[:, kb, :]
                    else:
                        at = (cb % 2) * P
                        stationary, moving = w_ih_cols[gate, pair][:, kb, at : at + P], x_all[:, kb, :]
                    nc.tensor.matmul(
                        accs[cb][sum_of(source, gate)][:],
                        stationary,
                        moving,
                        start=(sums[i] not in sums[:i]),
                        stop=(sums[i] not in sums[i + 1 :]),
                    )

            def finish_block(cb, acc):
                b_r = b_rz[:, cb : cb + 1]
                b_z = b_rz[:, BLOCKS + cb : BLOCKS + cb + 1]
                b_hn = bias_cols[:, rows + CAND * BLOCKS + cb : rows + CAND * BLOCKS + cb + 1]
                r = work.tile([P, N], F32, name="r")
                z = work.tile([P, N], F32, name="z")
                r_hn = work.tile([P, N], F32, name="r_hn")
                pre_cand = work.tile([P, N], F32, name="pre_cand")
                neg_cand = work.tile([P, N], F32, name="neg_cand")
                kept = work.tile([P, N], F32, name="kept")
                fresh = work.tile([P, N], F32, name="fresh")
                nc.scalar.activation(r[:], acc["r"][:], SIGMOID, bias=b_r)
                nc.vector.scalar_tensor_tensor(r_hn[:], acc["hn"][:], b_hn, r[:], op0=ADD, op1=MULT)
                nc.scalar.activation(z[:], acc["z"][:], SIGMOID, bias=b_z)
                nc.vector.tensor_tensor(kept[:], z[:], h_all[:, cb, :], MULT)
                halves = (slice(0, N // 2), slice(N // 2, N))
                for half in halves:
                    nc.vector.tensor_tensor(pre_cand[:, half], r_hn[:, half], acc["in"][:, half], ADD)
                    nc.scalar.activation(neg_cand[:, half], pre_cand[:, half], TANH, bias=neg_b_in[:, cb : cb + 1], scale=-1.0)
                for half in halves:
                    nc.vector.scalar_tensor_tensor(fresh[:, half], z[:, half], 1.0, neg_cand[:, half], op0=SUBTRACT, op1=MULT)
                nc.vector.tensor_tensor(windows[cb][:].indirect(offsets[:]), fresh[:], kept[:], ADD)
                nc.sync.dma_start(out[cb * P : (cb + 1) * P, :], windows[cb][:])

            for pair in range(BLOCKS // 2):
                accs = {cb: new_accumulators() for cb in (2 * pair, 2 * pair + 1)}
                multiply_pair(pair, accs)
                for cb in (2 * pair, 2 * pair + 1):
                    finish_block(cb, accs[cb])
